import numpy as np
import ml_dtypes

BF16 = ml_dtypes.bfloat16


def bf(x):
    return np.asarray(x, np.float32).astype(BF16)


def f32(x):
    return np.asarray(x, np.float32)


def f64(x):
    return np.asarray(x).astype(np.float64)


def striped(idx):
    return np.tile(idx.reshape(-1, 16).T, (8, 1))


S, D, M, N = 4096, 128, 256, 2048
MEM_SCALE = 2.0


def setup_inputs():
    return {"table": bf(np.sign(np.random.standard_normal((S, D)))), "memory": bf(MEM_SCALE * np.random.standard_normal((D, M))), "offs": striped(np.random.permutation(S)[:N])}


def reference(table, memory, offs):
    idx = offs[:16].T.reshape(-1)
    mem = f64(memory)
    z = f64(table)[idx].T
    rm = 1.0 / np.sqrt(np.sum(mem * mem, axis=0))
    sim = (mem.T @ z) * rm[:, None] / np.sqrt(D)
    e = np.exp(sim)
    return (mem @ e) / np.sum(e, axis=0, keepdims=True)

@@ -1,0 +1,130 @@
+import concourse.mybir as mybir
+from concourse.masks import make_identity
+
+P = 128
+S, D, M, N = 4096, 128, 256, 2048
+PIECE = 512
+N_PIECES = N // PIECE
+SLOT_BLOCKS = M // P
+ROW_BLOCKS = S // P
+BLOCKS_PER_BANK = 8
+N_CHUNKS = ROW_BLOCKS // BLOCKS_PER_BANK
+QUERY_BLOCKS = PIECE // P
+PAIR = 2
+BANK_F32 = 512
+
+FLOPS = 2 * M * D * N + 2 * D * M * N + 2 * M * N
+
+BF16, F32, U16 = mybir.dt.bfloat16, mybir.dt.float32, mybir.dt.uint16
+MULT, POW = mybir.AluOpType.mult, mybir.AluOpType.pow
+EXP = mybir.ActivationFunctionType.Exp
+
+
+def tile_memorymodule_kernel(tc, table, memory, offs, out):
+    nc = tc.nc
+    with (
+        tc.tile_pool(name="held", bufs=1) as held,
+        tc.tile_pool(name="exps", bufs=N_PIECES) as exps,
+        tc.tile_pool(name="work", bufs=2) as work,
+    ):
+        offsets = held.tile([P, N // 16], U16, name="offsets")
+        nc.sync.dma_start(offsets[:], offs)
+        mem_kn = held.tile([P, M], BF16, name="mem_kn")
+        nc.scalar.dma_start(mem_kn[:], memory)
+        rows = held.tile([P, ROW_BLOCKS, D], BF16, name="rows")
+        table_blocks = table.rearrange("(b p) k -> p b k", p=P)
+        for chunk in range(N_CHUNKS):
+            blocks = slice(chunk * BLOCKS_PER_BANK, (chunk + 1) * BLOCKS_PER_BANK)
+            queue = nc.sync if chunk % 2 == 0 else nc.scalar
+            queue.dma_start(rows[:, blocks, :], table_blocks[:, blocks, :])
+
+        identity = held.tile([P, P], BF16, name="identity")
+        make_identity(nc, identity[:])
+        identity_f32 = held.tile([P, P], F32, name="identity_f32")
+        make_identity(nc, identity_f32[:])
+        minus_half = held.tile([P, SLOT_BLOCKS], F32, name="minus_half")
+        nc.gpsimd.memset(minus_half[:], -0.5)
+
+        table_t = held.tile([P, S], BF16, name="table_t")
+        mem_nh1 = held.tile([P, SLOT_BLOCKS, D + 1], BF16, name="mem_nh1")
+        nc.vector.memset(mem_nh1[:], 1.0)
+        with tc.psum_pool(name="flip", bufs=2) as flip:
+            mem_flip = flip.tile([P, SLOT_BLOCKS, D], BF16, name="mem_flip")
+            for nb in range(SLOT_BLOCKS):
+                nc.tensor.transpose(mem_flip[:, nb, :], mem_kn[:, nb * P : (nb + 1) * P], identity[:])
+            nc.vector.tensor_copy(mem_nh1[:, :, 0:D], mem_flip[:])
+            squares = held.tile([P, SLOT_BLOCKS, D], F32, name="squares")
+            nc.vector.tensor_tensor(squares[:], mem_nh1[:, :, 0:D], mem_nh1[:, :, 0:D], MULT)
+            norm2 = held.tile([P, SLOT_BLOCKS], F32, name="norm2")
+            nc.vector.reduce_sum(norm2[:], squares[:], axis=mybir.AxisListType.X)
+            norm2_d = held.tile([P, SLOT_BLOCKS], F32, name="norm2_d")
+            nc.vector.tensor_scalar_mul(norm2_d[:], norm2[:], float(D))
+            sim_scale = held.tile([P, SLOT_BLOCKS], F32, name="sim_scale")
+            nc.gpsimd.tensor_tensor(sim_scale[:], norm2_d[:], minus_half[:], POW)
+
+            for chunk in range(N_CHUNKS):
+                bank = flip.tile([P, BLOCKS_PER_BANK * P], BF16, name="bank")
+                for i in range(BLOCKS_PER_BANK):
+                    nc.tensor.transpose(
+                        bank[:, i * P : (i + 1) * P], rows[:, chunk * BLOCKS_PER_BANK + i, :], identity[:]
+                    )
+                columns = slice(chunk * BLOCKS_PER_BANK * P, (chunk + 1) * BLOCKS_PER_BANK * P)
+                if chunk % 2 == 0:
+                    nc.vector.tensor_copy(table_t[:, columns], bank[:])
+                else:
+                    nc.scalar.copy(table_t[:, columns], bank[:])
+
+        with tc.psum_pool(name="psum", bufs=8) as psum:
+            e_of = []
+            for c in range(N_PIECES):
+                piece = offsets[:, c * (PIECE // 16) : (c + 1) * (PIECE // 16)]
+                e = exps.tile([P, SLOT_BLOCKS, PIECE], BF16, name="e")
+                for nb in range(SLOT_BLOCKS):
+                    sim = psum.tile([P, PIECE], F32, name="sim", tag="bank")
+                    nc.tensor.matmul(
+                        sim[:], mem_kn[:, nb * P : (nb + 1) * P], table_t[:].indirect(piece), start=True, stop=True
+                    )
+                    nc.scalar.activation(e[:, nb, :], sim[:], EXP, scale=sim_scale[:, nb : nb + 1])
+                e_of.append(e)
+
+            quotient_of = {}
+
+            def weighted_sum_and_divide(c):
+                e = e_of[c]
+                quotient = work.tile([P, QUERY_BLOCKS, D], F32, name="quotient")
+                for pair in range(QUERY_BLOCKS // PAIR):
+                    sums = psum.tile([P, PAIR, BANK_F32 // PAIR], F32, name="sums", tag="bank")
+                    for i in range(PAIR):
+                        qb = pair * PAIR + i
+                        for nb in range(SLOT_BLOCKS):
+                            nc.tensor.matmul(
+                                sums[:, i, 0 : D + 1],
+                                e[:, nb, qb * P : (qb + 1) * P],
+                                mem_nh1[:, nb, :],
+                                start=(nb == 0),
+                                stop=(nb == SLOT_BLOCKS - 1),
+                            )
+                    inverse = work.tile([P, PAIR, 1], F32, name="inverse")
+                    nc.vector.reciprocal(inverse[:], sums[:, :, D : D + 1])
+                    nc.vector.tensor_tensor(
+                        quotient[:, pair * PAIR : (pair + 1) * PAIR, :],
+                        sums[:, :, 0:D],
+                        inverse[:].to_broadcast([P, PAIR, D]),
+                        MULT,
+                    )
+                quotient_of[c] = quotient
+
+            def transpose_back_and_store(c):
+                quotient = quotient_of.pop(c)
+                flipped = psum.tile([P, PIECE], F32, name="flipped", tag="bank")
+                for qb in range(QUERY_BLOCKS):
+                    nc.tensor.transpose(flipped[:, qb * P : (qb + 1) * P], quotient[:, qb, :], identity_f32[:])
+                result = work.tile([P, PIECE], F32, name="result")
+                nc.scalar.copy(result[:], flipped[:])
+                nc.sync.dma_start(out[:, c * PIECE : (c + 1) * PIECE], result[:])
+
+            for step in range(N_PIECES + 1):
+                if step < N_PIECES:
+                    weighted_sum_and_divide(step)
+                if step >= 1:
+                    transpose_back_and_store(step - 1)

@@ -7,8 +7,8 @@ PIECE = 512
 N_PIECES = N // PIECE
 SLOT_BLOCKS = M // P
 ROW_BLOCKS = S // P
-BLOCKS_PER_BANK = 8
-N_CHUNKS = ROW_BLOCKS // BLOCKS_PER_BANK
+CHUNK_BLOCKS = 4
+N_CHUNKS = ROW_BLOCKS // CHUNK_BLOCKS
 QUERY_BLOCKS = PIECE // P
 PAIR = 2
 BANK_F32 = 512
@@ -34,9 +34,8 @@ def tile_memorymodule_kernel(tc, table, memory, offs, out):
         rows = held.tile([P, ROW_BLOCKS, D], BF16, name="rows")
         table_blocks = table.rearrange("(b p) k -> p b k", p=P)
         for chunk in range(N_CHUNKS):
-            blocks = slice(chunk * BLOCKS_PER_BANK, (chunk + 1) * BLOCKS_PER_BANK)
-            queue = nc.sync if chunk % 2 == 0 else nc.scalar
-            queue.dma_start(rows[:, blocks, :], table_blocks[:, blocks, :])
+            blocks = slice(chunk * CHUNK_BLOCKS, (chunk + 1) * CHUNK_BLOCKS)
+            nc.sync.dma_start(rows[:, blocks, :], table_blocks[:, blocks, :])
 
         identity = held.tile([P, P], BF16, name="identity")
         make_identity(nc, identity[:])
@@ -48,7 +47,7 @@ def tile_memorymodule_kernel(tc, table, memory, offs, out):
         table_t = held.tile([P, S], BF16, name="table_t")
         mem_nh1 = held.tile([P, SLOT_BLOCKS, D + 1], BF16, name="mem_nh1")
         nc.vector.memset(mem_nh1[:], 1.0)
-        with tc.psum_pool(name="flip", bufs=2) as flip:
+        with tc.psum_pool(name="flip", bufs=1) as flip:
             mem_flip = flip.tile([P, SLOT_BLOCKS, D], BF16, name="mem_flip")
             for nb in range(SLOT_BLOCKS):
                 nc.tensor.transpose(mem_flip[:, nb, :], mem_kn[:, nb * P : (nb + 1) * P], identity[:])
@@ -63,16 +62,14 @@ def tile_memorymodule_kernel(tc, table, memory, offs, out):
             nc.gpsimd.tensor_tensor(sim_scale[:], norm2_d[:], minus_half[:], POW)
 
             for chunk in range(N_CHUNKS):
-                bank = flip.tile([P, BLOCKS_PER_BANK * P], BF16, name="bank")
-                for i in range(BLOCKS_PER_BANK):
-                    nc.tensor.transpose(
-                        bank[:, i * P : (i + 1) * P], rows[:, chunk * BLOCKS_PER_BANK + i, :], identity[:]
-                    )
-                columns = slice(chunk * BLOCKS_PER_BANK * P, (chunk + 1) * BLOCKS_PER_BANK * P)
+                bank = flip.tile([P, CHUNK_BLOCKS * P], BF16, name="bank", bufs=N_CHUNKS - 1)
+                for i in range(CHUNK_BLOCKS):
+                    nc.tensor.transpose(bank[:, i * P : (i + 1) * P], rows[:, chunk * CHUNK_BLOCKS + i, :], identity[:])
+                columns = slice(chunk * CHUNK_BLOCKS * P, (chunk + 1) * CHUNK_BLOCKS * P)
                 if chunk % 2 == 0:
-                    nc.vector.tensor_copy(table_t[:, columns], bank[:])
-                else:
                     nc.scalar.copy(table_t[:, columns], bank[:])
+                else:
+                    nc.vector.tensor_copy(table_t[:, columns], bank[:])
 
         with tc.psum_pool(name="psum", bufs=8) as psum:
             e_of = []

@@ -12,6 +12,9 @@ N_CHUNKS = ROW_BLOCKS // CHUNK_BLOCKS
 QUERY_BLOCKS = PIECE // P
 PAIR = 2
 BANK_F32 = 512
+PAIRS_PER_PIECE = QUERY_BLOCKS // PAIR
+N_PAIRS = N_PIECES * PAIRS_PER_PIECE
+LAG = 2
 
 FLOPS = 2 * M * D * N + 2 * D * M * N + 2 * M * N
 
@@ -25,7 +28,7 @@ def tile_memorymodule_kernel(tc, table, memory, offs, out):
     with (
         tc.tile_pool(name="held", bufs=1) as held,
         tc.tile_pool(name="exps", bufs=N_PIECES) as exps,
-        tc.tile_pool(name="work", bufs=2) as work,
+        tc.tile_pool(name="work", bufs=LAG + 2) as work,
     ):
         offsets = held.tile([P, N // 16], U16, name="offsets")
         nc.sync.dma_start(offsets[:], offs)
@@ -45,6 +48,7 @@ def tile_memorymodule_kernel(tc, table, memory, offs, out):
         nc.gpsimd.memset(minus_half[:], -0.5)
 
         table_t = held.tile([P, S], BF16, name="table_t")
+        result = held.tile([P, N], F32, name="result")
         mem_nh1 = held.tile([P, SLOT_BLOCKS, D + 1], BF16, name="mem_nh1")
         nc.vector.memset(mem_nh1[:], 1.0)
         with tc.psum_pool(name="flip", bufs=1) as flip:
@@ -86,42 +90,37 @@ def tile_memorymodule_kernel(tc, table, memory, offs, out):
 
             quotient_of = {}
 
-            def weighted_sum_and_divide(c):
+            def weighted_sum_and_divide(pair):
+                c, half = divmod(pair, PAIRS_PER_PIECE)
                 e = e_of[c]
-                quotient = work.tile([P, QUERY_BLOCKS, D], F32, name="quotient")
-                for pair in range(QUERY_BLOCKS // PAIR):
-                    sums = psum.tile([P, PAIR, BANK_F32 // PAIR], F32, name="sums", tag="bank")
-                    for i in range(PAIR):
-                        qb = pair * PAIR + i
-                        for nb in range(SLOT_BLOCKS):
-                            nc.tensor.matmul(
-                                sums[:, i, 0 : D + 1],
-                                e[:, nb, qb * P : (qb + 1) * P],
-                                mem_nh1[:, nb, :],
-                                start=(nb == 0),
-                                stop=(nb == SLOT_BLOCKS - 1),
-                            )
-                    inverse = work.tile([P, PAIR, 1], F32, name="inverse")
-                    nc.vector.reciprocal(inverse[:], sums[:, :, D : D + 1])
-                    nc.vector.tensor_tensor(
-                        quotient[:, pair * PAIR : (pair + 1) * PAIR, :],
-                        sums[:, :, 0:D],
-                        inverse[:].to_broadcast([P, PAIR, D]),
-                        MULT,
-                    )
-                quotient_of[c] = quotient
+                sums = psum.tile([P, PAIR, BANK_F32 // PAIR], F32, name="sums", tag="bank")
+                for i in range(PAIR):
+                    first = (half * PAIR + i) * P
+                    for nb in range(SLOT_BLOCKS):
+                        nc.tensor.matmul(
+                            sums[:, i, 0 : D + 1],
+                            e[:, nb, first : first + P],
+                            mem_nh1[:, nb, :],
+                            start=(nb == 0),
+                            stop=(nb == SLOT_BLOCKS - 1),
+                        )
+                inverse = work.tile([P, PAIR, 1], F32, name="inverse")
+                nc.vector.reciprocal(inverse[:], sums[:, :, D : D + 1])
+                quotient = work.tile([P, PAIR, D], F32, name="quotient")
+                nc.vector.tensor_tensor(quotient[:], sums[:, :, 0:D], inverse[:].to_broadcast([P, PAIR, D]), MULT)
+                quotient_of[pair] = quotient
 
-            def transpose_back_and_store(c):
-                quotient = quotient_of.pop(c)
-                flipped = psum.tile([P, PIECE], F32, name="flipped", tag="bank")
-                for qb in range(QUERY_BLOCKS):
-                    nc.tensor.transpose(flipped[:, qb * P : (qb + 1) * P], quotient[:, qb, :], identity_f32[:])
-                result = work.tile([P, PIECE], F32, name="result")
-                nc.scalar.copy(result[:], flipped[:])
-                nc.sync.dma_start(out[:, c * PIECE : (c + 1) * PIECE], result[:])
+            def transpose_back_and_store(pair):
+                quotient = quotient_of.pop(pair)
+                flipped = psum.tile([P, PAIR * P], F32, name="flipped", tag="bank")
+                for i in range(PAIR):
+                    nc.tensor.transpose(flipped[:, i * P : (i + 1) * P], quotient[:, i, :], identity_f32[:])
+                queries = slice(pair * PAIR * P, (pair + 1) * PAIR * P)
+                nc.scalar.copy(result[:, queries], flipped[:])
+                nc.sync.dma_start(out[:, queries], result[:, queries])
 
-            for step in range(N_PIECES + 1):
-                if step < N_PIECES:
+            for step in range(N_PAIRS + LAG):
+                if step < N_PAIRS:
                     weighted_sum_and_divide(step)
-                if step >= 1:
-                    transpose_back_and_store(step - 1)
+                if step >= LAG:
+                    transpose_back_and_store(step - LAG)

@@ -14,7 +14,6 @@ PAIR = 2
 BANK_F32 = 512
 PAIRS_PER_PIECE = QUERY_BLOCKS // PAIR
 N_PAIRS = N_PIECES * PAIRS_PER_PIECE
-LAG = 2
 
 FLOPS = 2 * M * D * N + 2 * D * M * N + 2 * M * N
 
@@ -28,7 +27,7 @@ def tile_memorymodule_kernel(tc, table, memory, offs, out):
     with (
         tc.tile_pool(name="held", bufs=1) as held,
         tc.tile_pool(name="exps", bufs=N_PIECES) as exps,
-        tc.tile_pool(name="work", bufs=LAG + 2) as work,
+        tc.tile_pool(name="quotients", bufs=N_PAIRS) as quotients,
     ):
         offsets = held.tile([P, N // 16], U16, name="offsets")
         nc.sync.dma_start(offsets[:], offs)
@@ -88,9 +87,8 @@ def tile_memorymodule_kernel(tc, table, memory, offs, out):
                     nc.scalar.activation(e[:, nb, :], sim[:], EXP, scale=sim_scale[:, nb : nb + 1])
                 e_of.append(e)
 
-            quotient_of = {}
-
-            def weighted_sum_and_divide(pair):
+            quotient_of = []
+            for pair in range(N_PAIRS):
                 c, half = divmod(pair, PAIRS_PER_PIECE)
                 e = e_of[c]
                 sums = psum.tile([P, PAIR, BANK_F32 // PAIR], F32, name="sums", tag="bank")
@@ -104,23 +102,16 @@ def tile_memorymodule_kernel(tc, table, memory, offs, out):
                             start=(nb == 0),
                             stop=(nb == SLOT_BLOCKS - 1),
                         )
-                inverse = work.tile([P, PAIR, 1], F32, name="inverse")
+                inverse = quotients.tile([P, PAIR, 1], F32, name="inverse")
                 nc.vector.reciprocal(inverse[:], sums[:, :, D : D + 1])
-                quotient = work.tile([P, PAIR, D], F32, name="quotient")
+                quotient = quotients.tile([P, PAIR, D], F32, name="quotient")
                 nc.vector.tensor_tensor(quotient[:], sums[:, :, 0:D], inverse[:].to_broadcast([P, PAIR, D]), MULT)
-                quotient_of[pair] = quotient
+                quotient_of.append(quotient)
 
-            def transpose_back_and_store(pair):
-                quotient = quotient_of.pop(pair)
+            for pair in range(N_PAIRS):
                 flipped = psum.tile([P, PAIR * P], F32, name="flipped", tag="bank")
                 for i in range(PAIR):
-                    nc.tensor.transpose(flipped[:, i * P : (i + 1) * P], quotient[:, i, :], identity_f32[:])
+                    nc.tensor.transpose(flipped[:, i * P : (i + 1) * P], quotient_of[pair][:, i, :], identity_f32[:])
                 queries = slice(pair * PAIR * P, (pair + 1) * PAIR * P)
                 nc.scalar.copy(result[:, queries], flipped[:])
                 nc.sync.dma_start(out[:, queries], result[:, queries])
-
-            for step in range(N_PAIRS + LAG):
-                if step < N_PAIRS:
-                    weighted_sum_and_divide(step)
-                if step >= LAG:
-                    transpose_back_and_store(step - LAG)

@@ -15,6 +15,9 @@ BANK_F32 = 512
 PAIRS_PER_PIECE = QUERY_BLOCKS // PAIR
 N_PAIRS = N_PIECES * PAIRS_PER_PIECE
 
+WARM_UP = 5
+KEEP_WARM = 256
+
 FLOPS = 2 * M * D * N + 2 * D * M * N + 2 * M * N
 
 BF16, F32, U16 = mybir.dt.bfloat16, mybir.dt.float32, mybir.dt.uint16
@@ -45,12 +48,18 @@ def tile_memorymodule_kernel(tc, table, memory, offs, out):
         make_identity(nc, identity_f32[:])
         minus_half = held.tile([P, SLOT_BLOCKS], F32, name="minus_half")
         nc.gpsimd.memset(minus_half[:], -0.5)
+        zeros = held.tile([P, PIECE], BF16, name="zeros")
+        nc.vector.memset(zeros[:], 0.0)
 
         table_t = held.tile([P, S], BF16, name="table_t")
         result = held.tile([P, N], F32, name="result")
         mem_nh1 = held.tile([P, SLOT_BLOCKS, D + 1], BF16, name="mem_nh1")
         nc.vector.memset(mem_nh1[:], 1.0)
         with tc.psum_pool(name="flip", bufs=1) as flip:
+            idle = flip.tile([P, PIECE], F32, name="idle")
+            for i in range(WARM_UP):
+                nc.tensor.matmul(idle[:], identity[:], zeros[:], start=True, stop=True)
+
             mem_flip = flip.tile([P, SLOT_BLOCKS, D], BF16, name="mem_flip")
             for nb in range(SLOT_BLOCKS):
                 nc.tensor.transpose(mem_flip[:, nb, :], mem_kn[:, nb * P : (nb + 1) * P], identity[:])
@@ -65,9 +74,17 @@ def tile_memorymodule_kernel(tc, table, memory, offs, out):
             nc.gpsimd.tensor_tensor(sim_scale[:], norm2_d[:], minus_half[:], POW)
 
             for chunk in range(N_CHUNKS):
-                bank = flip.tile([P, CHUNK_BLOCKS * P], BF16, name="bank", bufs=N_CHUNKS - 1)
+                bank = flip.tile([P, CHUNK_BLOCKS * P], BF16, name="bank", bufs=N_CHUNKS - 2)
                 for i in range(CHUNK_BLOCKS):
                     nc.tensor.transpose(bank[:, i * P : (i + 1) * P], rows[:, chunk * CHUNK_BLOCKS + i, :], identity[:])
+                first_block = chunk * CHUNK_BLOCKS
+                nc.tensor.matmul(
+                    idle[:, 0:KEEP_WARM],
+                    identity[:],
+                    rows[:, first_block : first_block + KEEP_WARM // D, :].rearrange("p b k -> p (b k)"),
+                    start=True,
+                    stop=True,
+                )
                 columns = slice(chunk * CHUNK_BLOCKS * P, (chunk + 1) * CHUNK_BLOCKS * P)
                 if chunk % 2 == 0:
                     nc.scalar.copy(table_t[:, columns], bank[:])

@@ -36,11 +36,10 @@ def tile_memorymodule_kernel(tc, table, memory, offs, out):
         nc.sync.dma_start(offsets[:], offs)
         mem_kn = held.tile([P, M], BF16, name="mem_kn")
         nc.scalar.dma_start(mem_kn[:], memory)
-        rows = held.tile([P, ROW_BLOCKS, D], BF16, name="rows")
-        table_blocks = table.rearrange("(b p) k -> p b k", p=P)
+        rows = held.tile([P, N_CHUNKS, CHUNK_BLOCKS, D], BF16, name="rows")
+        table_chunks = table.rearrange("(c p r) k -> p c r k", p=P, r=CHUNK_BLOCKS)
         for chunk in range(N_CHUNKS):
-            blocks = slice(chunk * CHUNK_BLOCKS, (chunk + 1) * CHUNK_BLOCKS)
-            nc.sync.dma_start(rows[:, blocks, :], table_blocks[:, blocks, :])
+            nc.sync.dma_start(rows[:, chunk, :, :], table_chunks[:, chunk, :, :])
 
         identity = held.tile([P, P], BF16, name="identity")
         make_identity(nc, identity[:])
@@ -74,22 +73,22 @@ def tile_memorymodule_kernel(tc, table, memory, offs, out):
             nc.gpsimd.tensor_tensor(sim_scale[:], norm2_d[:], minus_half[:], POW)
 
             for chunk in range(N_CHUNKS):
-                bank = flip.tile([P, CHUNK_BLOCKS * P], BF16, name="bank", bufs=N_CHUNKS - 2)
-                for i in range(CHUNK_BLOCKS):
-                    nc.tensor.transpose(bank[:, i * P : (i + 1) * P], rows[:, chunk * CHUNK_BLOCKS + i, :], identity[:])
-                first_block = chunk * CHUNK_BLOCKS
+                bank = flip.tile([P, CHUNK_BLOCKS, P], BF16, name="bank", bufs=N_CHUNKS - 2)
+                for r in range(CHUNK_BLOCKS):
+                    nc.tensor.transpose(bank[:, r, :], rows[:, chunk, r, :], identity[:])
                 nc.tensor.matmul(
                     idle[:, 0:KEEP_WARM],
                     identity[:],
-                    rows[:, first_block : first_block + KEEP_WARM // D, :].rearrange("p b k -> p (b k)"),
+                    rows[:, chunk, 0 : KEEP_WARM // D, :].rearrange("p r k -> p (r k)"),
                     start=True,
                     stop=True,
                 )
-                columns = slice(chunk * CHUNK_BLOCKS * P, (chunk + 1) * CHUNK_BLOCKS * P)
+                columns = table_t[:, chunk * CHUNK_BLOCKS * P : (chunk + 1) * CHUNK_BLOCKS * P]
+                in_row_order = bank[:].rearrange("k r p -> k p r")
                 if chunk % 2 == 0:
-                    nc.scalar.copy(table_t[:, columns], bank[:])
+                    nc.scalar.copy(columns.rearrange("k (p r) -> k p r", r=CHUNK_BLOCKS), in_row_order)
                 else:
-                    nc.vector.tensor_copy(table_t[:, columns], bank[:])
+                    nc.vector.tensor_copy(columns.rearrange("k (p r) -> k p r", r=CHUNK_BLOCKS), in_row_order)
 
         with tc.psum_pool(name="psum", bufs=8) as psum:
             e_of = []

@@ -16,7 +16,6 @@ PAIRS_PER_PIECE = QUERY_BLOCKS // PAIR
 N_PAIRS = N_PIECES * PAIRS_PER_PIECE
 
 WARM_UP = 5
-KEEP_WARM = 256
 
 FLOPS = 2 * M * D * N + 2 * D * M * N + 2 * M * N
 
@@ -76,13 +75,6 @@ def tile_memorymodule_kernel(tc, table, memory, offs, out):
                 bank = flip.tile([P, CHUNK_BLOCKS, P], BF16, name="bank", bufs=N_CHUNKS - 2)
                 for r in range(CHUNK_BLOCKS):
                     nc.tensor.transpose(bank[:, r, :], rows[:, chunk, r, :], identity[:])
-                nc.tensor.matmul(
-                    idle[:, 0:KEEP_WARM],
-                    identity[:],
-                    rows[:, chunk, 0 : KEEP_WARM // D, :].rearrange("p r k -> p (r k)"),
-                    start=True,
-                    stop=True,
-                )
                 columns = table_t[:, chunk * CHUNK_BLOCKS * P : (chunk + 1) * CHUNK_BLOCKS * P]
                 in_row_order = bank[:].rearrange("k r p -> k p r")
                 if chunk % 2 == 0:

@@ -15,7 +15,8 @@ BANK_F32 = 512
 PAIRS_PER_PIECE = QUERY_BLOCKS // PAIR
 N_PAIRS = N_PIECES * PAIRS_PER_PIECE
 
-WARM_UP = 5
+WARM_UP = 4
+KEEP_WARM = 256
 
 FLOPS = 2 * M * D * N + 2 * D * M * N + 2 * M * N
 
@@ -75,6 +76,13 @@ def tile_memorymodule_kernel(tc, table, memory, offs, out):
                 bank = flip.tile([P, CHUNK_BLOCKS, P], BF16, name="bank", bufs=N_CHUNKS - 2)
                 for r in range(CHUNK_BLOCKS):
                     nc.tensor.transpose(bank[:, r, :], rows[:, chunk, r, :], identity[:])
+                nc.tensor.matmul(
+                    idle[:, 0:KEEP_WARM],
+                    identity[:],
+                    rows[:, chunk, 0 : KEEP_WARM // D, :].rearrange("p r k -> p (r k)"),
+                    start=True,
+                    stop=True,
+                )
                 columns = table_t[:, chunk * CHUNK_BLOCKS * P : (chunk + 1) * CHUNK_BLOCKS * P]
                 in_row_order = bank[:].rearrange("k r p -> k p r")
                 if chunk % 2 == 0:

import concourse.mybir as mybir
from concourse.masks import make_identity

P = 128
S, D, M, N = 4096, 128, 256, 2048
PIECE = 512
N_PIECES = N // PIECE
SLOT_BLOCKS = M // P
ROW_BLOCKS = S // P
CHUNK_BLOCKS = 4
N_CHUNKS = ROW_BLOCKS // CHUNK_BLOCKS
QUERY_BLOCKS = PIECE // P
PAIR = 2
BANK_F32 = 512
PAIRS_PER_PIECE = QUERY_BLOCKS // PAIR
N_PAIRS = N_PIECES * PAIRS_PER_PIECE

WARM_UP = 4
KEEP_WARM = 256

FLOPS = 2 * M * D * N + 2 * D * M * N + 2 * M * N

BF16, F32, U16 = mybir.dt.bfloat16, mybir.dt.float32, mybir.dt.uint16
MULT, POW = mybir.AluOpType.mult, mybir.AluOpType.pow
EXP = mybir.ActivationFunctionType.Exp


def tile_memorymodule_kernel(tc, table, memory, offs, out):
    nc = tc.nc
    with (
        tc.tile_pool(name="held", bufs=1) as held,
        tc.tile_pool(name="exps", bufs=N_PIECES) as exps,
        tc.tile_pool(name="quotients", bufs=N_PAIRS) as quotients,
    ):
        offsets = held.tile([P, N // 16], U16, name="offsets")
        nc.sync.dma_start(offsets[:], offs)
        mem_kn = held.tile([P, M], BF16, name="mem_kn")
        nc.scalar.dma_start(mem_kn[:], memory)
        rows = held.tile([P, N_CHUNKS, CHUNK_BLOCKS, D], BF16, name="rows")
        table_chunks = table.rearrange("(c p r) k -> p c r k", p=P, r=CHUNK_BLOCKS)
        for chunk in range(N_CHUNKS):
            nc.sync.dma_start(rows[:, chunk, :, :], table_chunks[:, chunk, :, :])

        identity = held.tile([P, P], BF16, name="identity")
        make_identity(nc, identity[:])
        identity_f32 = held.tile([P, P], F32, name="identity_f32")
        make_identity(nc, identity_f32[:])
        minus_half = held.tile([P, SLOT_BLOCKS], F32, name="minus_half")
        nc.gpsimd.memset(minus_half[:], -0.5)
        zeros = held.tile([P, PIECE], BF16, name="zeros")
        nc.vector.memset(zeros[:], 0.0)

        table_t = held.tile([P, S], BF16, name="table_t")
        result = held.tile([P, N], F32, name="result")
        mem_nh1 = held.tile([P, SLOT_BLOCKS, D + 1], BF16, name="mem_nh1")
        nc.vector.memset(mem_nh1[:], 1.0)
        with tc.psum_pool(name="flip", bufs=1) as flip:
            idle = flip.tile([P, PIECE], F32, name="idle")
            for i in range(WARM_UP):
                nc.tensor.matmul(idle[:], identity[:], zeros[:], start=True, stop=True)

            mem_flip = flip.tile([P, SLOT_BLOCKS, D], BF16, name="mem_flip")
            for nb in range(SLOT_BLOCKS):
                nc.tensor.transpose(mem_flip[:, nb, :], mem_kn[:, nb * P : (nb + 1) * P], identity[:])
            nc.vector.tensor_copy(mem_nh1[:, :, 0:D], mem_flip[:])
            squares = held.tile([P, SLOT_BLOCKS, D], F32, name="squares")
            nc.vector.tensor_tensor(squares[:], mem_nh1[:, :, 0:D], mem_nh1[:, :, 0:D], MULT)
            norm2 = held.tile([P, SLOT_BLOCKS], F32, name="norm2")
            nc.vector.reduce_sum(norm2[:], squares[:], axis=mybir.AxisListType.X)
            norm2_d = held.tile([P, SLOT_BLOCKS], F32, name="norm2_d")
            nc.vector.tensor_scalar_mul(norm2_d[:], norm2[:], float(D))
            sim_scale = held.tile([P, SLOT_BLOCKS], F32, name="sim_scale")
            nc.gpsimd.tensor_tensor(sim_scale[:], norm2_d[:], minus_half[:], POW)

            for chunk in range(N_CHUNKS):
                bank = flip.tile([P, CHUNK_BLOCKS, P], BF16, name="bank", bufs=N_CHUNKS - 2)
                for r in range(CHUNK_BLOCKS):
                    nc.tensor.transpose(bank[:, r, :], rows[:, chunk, r, :], identity[:])
                nc.tensor.matmul(
                    idle[:, 0:KEEP_WARM],
                    identity[:],
                    rows[:, chunk, 0 : KEEP_WARM // D, :].rearrange("p r k -> p (r k)"),
                    start=True,
                    stop=True,
                )
                columns = table_t[:, chunk * CHUNK_BLOCKS * P : (chunk + 1) * CHUNK_BLOCKS * P]
                in_row_order = bank[:].rearrange("k r p -> k p r")
                if chunk % 2 == 0:
                    nc.scalar.copy(columns.rearrange("k (p r) -> k p r", r=CHUNK_BLOCKS), in_row_order)
                else:
                    nc.vector.tensor_copy(columns.rearrange("k (p r) -> k p r", r=CHUNK_BLOCKS), in_row_order)

        with tc.psum_pool(name="psum", bufs=8) as psum:
            e_of = []
            for c in range(N_PIECES):
                piece = offsets[:, c * (PIECE // 16) : (c + 1) * (PIECE // 16)]
                e = exps.tile([P, SLOT_BLOCKS, PIECE], BF16, name="e")
                for nb in range(SLOT_BLOCKS):
                    sim = psum.tile([P, PIECE], F32, name="sim", tag="bank")
                    nc.tensor.matmul(
                        sim[:], mem_kn[:, nb * P : (nb + 1) * P], table_t[:].indirect(piece), start=True, stop=True
                    )
                    nc.scalar.activation(e[:, nb, :], sim[:], EXP, scale=sim_scale[:, nb : nb + 1])
                e_of.append(e)

            quotient_of = []
            for pair in range(N_PAIRS):
                c, half = divmod(pair, PAIRS_PER_PIECE)
                e = e_of[c]
                sums = psum.tile([P, PAIR, BANK_F32 // PAIR], F32, name="sums", tag="bank")
                for i in range(PAIR):
                    first = (half * PAIR + i) * P
                    for nb in range(SLOT_BLOCKS):
                        nc.tensor.matmul(
                            sums[:, i, 0 : D + 1],
                            e[:, nb, first : first + P],
                            mem_nh1[:, nb, :],
                            start=(nb == 0),
                            stop=(nb == SLOT_BLOCKS - 1),
                        )
                inverse = quotients.tile([P, PAIR, 1], F32, name="inverse")
                nc.vector.reciprocal(inverse[:], sums[:, :, D : D + 1])
                quotient = quotients.tile([P, PAIR, D], F32, name="quotient")
                nc.vector.tensor_tensor(quotient[:], sums[:, :, 0:D], inverse[:].to_broadcast([P, PAIR, D]), MULT)
                quotient_of.append(quotient)

            for pair in range(N_PAIRS):
                flipped = psum.tile([P, PAIR * P], F32, name="flipped", tag="bank")
                for i in range(PAIR):
                    nc.tensor.transpose(flipped[:, i * P : (i + 1) * P], quotient_of[pair][:, i, :], identity_f32[:])
                queries = slice(pair * PAIR * P, (pair + 1) * PAIR * P)
                nc.scalar.copy(result[:, queries], flipped[:])
                nc.sync.dma_start(out[:, queries], result[:, queries])
